import numpy as np
import ml_dtypes


def mxq(x, axis, fmt="e4m3"):
    dtype, down = {"e4m3": (ml_dtypes.float8_e4m3fn, 7), "e5m2": (ml_dtypes.float8_e5m2, 14)}[fmt]
    v = np.moveaxis(np.asarray(x, np.float32).astype(ml_dtypes.bfloat16).astype(np.float64), axis, -1)
    blocks = v.reshape(v.shape[:-1] + (-1, 32))
    amax = np.abs(blocks).max(-1, keepdims=True)
    byte = np.maximum(np.where(amax > 0, np.frexp(amax)[1] - 1 + 127, 0) - down, 1)
    scale = np.exp2(byte - 127.0)
    codes = (blocks / scale).astype(np.float32).astype(dtype).astype(np.float64)
    return np.moveaxis((codes * scale).reshape(v.shape), -1, axis)


WIDE = False


def mx_kscale(k):
    if not WIDE:
        return np.ones(k)
    levels = np.array([10, -10, 5, -5, 0])
    if k % 512:
        return np.exp2(np.random.permutation(np.resize(levels, k // 32))).repeat(32)
    a = np.empty((k // 512, 16))
    for p in range(k // 512):
        a[p, :8] = np.random.permutation(np.resize(levels, 8))
        for g in range(8):
            far = levels[np.abs(levels - a[p, g]) >= 10]
            a[p, g + 8] = far[np.random.randint(len(far))]
    return np.exp2(a.ravel()).repeat(32)


BF16 = ml_dtypes.bfloat16


def bf(x):
    return np.asarray(x, np.float32).astype(BF16)


def f64(x):
    return np.asarray(x).astype(np.float64)


H, A, NS, NE, M = 1024, 1024, 1024, 512, 1024


def draw0():
    s, t = mx_kscale(H), mx_kscale(H)
    wsc = 0.25 / np.sqrt(H)
    return {
        "attendee_stmts": bf(np.random.standard_normal((NS, H)) * s),
        "attendee_eres": bf(np.random.standard_normal((NE, H)) * s),
        "attender": bf(np.random.standard_normal((M, H)) * 0.2 / t),
        "W_ss": bf(np.random.standard_normal((H, H)) * wsc * t[:, None] / s),
        "b_ss": bf(np.random.standard_normal(H) * 0.1 * t),
        "W_es": bf(np.random.standard_normal((H, H)) * wsc * t[:, None] / s),
        "b_es": bf(np.random.standard_normal(H) * 0.1 * t),
    }


def core(attendee_stmts, attendee_eres, attender, W_ss, b_ss, W_es, b_es):
    aq = mxq(f64(attender), 1, "e4m3")
    p_ss = (mxq(f64(attendee_stmts), 1, "e4m3") @ mxq(f64(W_ss), 1, "e4m3").T) + f64(b_ss)
    p_es = (mxq(f64(attendee_eres), 1, "e4m3") @ mxq(f64(W_es), 1, "e4m3").T) + f64(b_es)
    scores_ss = mxq(p_ss, 1, "e4m3") @ aq.T
    scores_es = mxq(p_es, 1, "e4m3") @ aq.T
    return scores_ss, scores_es


def e4m3fn_bytes(y):
    return np.clip(np.asarray(y, np.float64), -448.0, 448.0).astype(np.float32).astype(ml_dtypes.float8_e4m3fn).view(np.uint8)


def e4m3fn_values(b):
    return np.asarray(b, np.uint8).view(ml_dtypes.float8_e4m3fn).astype(np.float64)


def setup_inputs():
    d = draw0()
    x0 = np.asarray(d['attender']).astype(np.float64)
    s = (np.max(np.abs(x0), axis=(0,), keepdims=True) / 448.0).astype(np.float32)
    out = {}
    for k, v in d.items():
        if k == 'attender':
            out['attender_bytes'] = e4m3fn_bytes(x0 / s.astype(np.float64))
            out['attender_scale'] = s
        else:
            out[k] = v
    return out


def reference(attendee_stmts, attendee_eres, attender_bytes, attender_scale, W_ss, b_ss, W_es, b_es):
    return core(attendee_stmts, attendee_eres, e4m3fn_values(attender_bytes) * attender_scale.astype(np.float64), W_ss, b_ss, W_es, b_es)

@@ -1,0 +1,288 @@
+from contextlib import ExitStack
+
+import concourse.mybir as mybir
+from concourse.masks import make_identity
+
+H, NS, NE, M = 1024, 1024, 512, 1024
+FLOPS = 2 * (NS + NE) * H * H + 2 * (NS + NE) * M * H
+
+F32 = mybir.dt.float32
+BF16 = mybir.dt.bfloat16
+U32 = mybir.dt.uint32
+U8 = mybir.dt.uint8
+FP8 = mybir.dt.float8_e4m3fn
+FP8X4 = mybir.dt.float8_e4m3fn_x4
+ADD = mybir.AluOpType.add
+MULT = mybir.AluOpType.mult
+
+P = 128
+T = 4
+G = H // (P * T)
+U = 2
+N2 = 512
+HALVES = M // N2
+S_TILES = NS // P
+E_TILES = NE // P
+TILES = S_TILES + E_TILES
+
+
+def tile_attention_pa_kernel(
+    tc, attendee_stmts, attendee_eres, attender_bytes, attender_scale, W_ss, b_ss, W_es, b_es, out_0, out_1
+):
+    nc = tc.nc
+    with ExitStack() as ctx:
+        keep = ctx.enter_context(tc.tile_pool(name="keep", bufs=1))
+        wide = ctx.enter_context(tc.tile_pool(name="wide", bufs=4))
+        ordered_pool = ctx.enter_context(tc.tile_pool(name="ordered_pool", bufs=6))
+        sums = ctx.enter_context(tc.tile_pool(name="sums", bufs=3))
+        results = ctx.enter_context(tc.tile_pool(name="results", bufs=4))
+        turn_psum = ctx.enter_context(tc.psum_pool(name="turn_psum", bufs=3))
+        first_psum = ctx.enter_context(tc.psum_pool(name="first_psum", bufs=2))
+        second_psum = ctx.enter_context(tc.psum_pool(name="second_psum", bufs=3))
+        ctx.enter_context(tc.manual_schedule())
+
+        ident = keep.tile([P, P], F32, name="ident")
+        make_identity(nc, ident[:])
+
+        scale = keep.tile([P, G, T], F32, name="scale")
+        nc.scalar.dma_start(out=scale[:], in_=attender_scale.rearrange("o (g p t) -> p (o g) t", g=G, p=P, t=T))
+        bias = []
+        for name, vec in (("bias_ss", b_ss), ("bias_es", b_es)):
+            b = keep.tile([P, G, T], BF16, name=name)
+            nc.scalar.dma_start(out=b[:], in_=vec.rearrange("(g p t) -> p g t", g=G, p=P, t=T))
+            bias.append(b)
+
+        codes_raw = keep.tile([P, M // P, H], U8, name="codes_raw")
+        bytes_view = attender_bytes.rearrange("(j p) k -> p j k", p=P)
+        w_raw = []
+        w_view = []
+        for name, w in (("w_ss_raw", W_ss), ("w_es_raw", W_es)):
+            raw = keep.tile([P, G * T, H], BF16, name=name)
+            w_raw.append(raw)
+            w_view.append(w.rearrange("(g m t) k -> m g t k", g=G, m=P, t=T))
+        x_raw = keep.tile([P, TILES, H], BF16, name="x_raw")
+        s_view = attendee_stmts.rearrange("(q p e) k -> p q e k", p=P, e=2)
+        e_view = attendee_eres.rearrange("(q p e) k -> p q e k", p=P, e=2)
+
+        def load_bytes(j, n):
+            nc.sync.dma_start(out=codes_raw[:, j : j + n, :], in_=bytes_view[:, j : j + n, :])
+
+        def load_weight(w, j, n):
+            nc.sync.dma_start(out=w_raw[w][:, j : j + n, :], in_=w_view[w][:, j // T, j % T : j % T + n, :])
+
+        def load_rows(i):
+            view = s_view[:, i // 2] if i < S_TILES else e_view[:, (i - S_TILES) // 2]
+            nc.sync.dma_start(out=x_raw[:, i : i + 2, :], in_=view)
+
+        load_weight(0, 0, 1)
+        load_bytes(0, 2)
+        load_weight(0, 1, 1)
+        load_weight(0, 2, 2)
+        load_bytes(2, 2)
+        load_weight(0, 4, 2)
+        load_weight(0, 6, 2)
+        load_rows(0)
+        load_bytes(4, 4)
+        load_rows(2)
+        load_weight(1, 0, 2)
+        load_rows(4)
+        load_weight(1, 2, 2)
+        load_weight(1, 4, 2)
+        load_rows(6)
+        load_weight(1, 6, 2)
+        load_rows(8)
+        load_rows(10)
+
+        def quantised(name, words):
+            codes = keep.tile([P, words], U32, name=name + "_codes", align_bytes=64)
+            planes = keep.tile([P, words], U8, name=name + "_scales", align_bytes=64)
+            return codes, planes
+
+        w_q = [[quantised("w%d_%d" % (w, j), G * P) for j in range(G * T)] for w in range(2)]
+        x_q = [quantised("x_%d" % i, G * P) for i in range(TILES)]
+        p_q = [quantised("p_%d" % i, G * P) for i in range(TILES)]
+        a_q = [[quantised("a_%d_%d" % (h, g), N2) for g in range(G)] for h in range(HALVES)]
+        a_wide = [keep.tile([P, G, N2, T], BF16, name="a_wide_%d" % h, align_bytes=64) for h in range(HALVES)]
+        a_rows = [keep.tile([P, H], BF16, name="a_rows_%d" % j) for j in range(M // P)]
+
+        def quantise(dst, src):
+            nc.vector.quantize_mx(out=dst[0][:].bitcast(FP8X4), scales=dst[1][:], in_=src)
+
+        def turn(rows):
+            bank = turn_psum.tile([P, G * U * P], F32, name="turned")
+            words = rows.bitcast(F32)
+            for g in range(G):
+                for u in range(U):
+                    c = (g * U + u) * P
+                    nc.tensor.transpose(bank[:, c : c + P], words[:, 256 * g + u : 256 * (g + 1) : U], ident[:])
+            return bank
+
+        def turn_sorted(rows):
+            bank = turn_psum.tile([P, G * U * P], F32, name="turned")
+            words = rows.bitcast(F32)
+            for c in range(0, G * U * P, P):
+                nc.tensor.transpose(bank[:, c : c + P], words[:, c : c + P], ident[:])
+            return bank
+
+        def sort_words(engine, rows):
+            ordered = ordered_pool.tile([P, H], BF16, name="ordered")
+            (nc.vector.tensor_copy if engine == "V" else nc.scalar.copy)(
+                out=ordered[:].bitcast(F32).rearrange("p (g u q) -> p g u q", g=G, u=U),
+                in_=rows.bitcast(F32).rearrange("p (g q u) -> p g u q", g=G, u=U),
+            )
+            return ordered
+
+        def turn_plain(key, rows):
+            bank = turn_sorted(sorted_rows.pop(key)[:]) if key in sorted_rows else turn(rows)
+            grouped = wide.tile([P, G * P * T], BF16, name="grouped", align_bytes=64)
+            nc.scalar.copy(
+                out=grouped[:].bitcast(F32).rearrange("p (g r u) -> p g r u", g=G, u=U),
+                in_=bank[:].rearrange("p (g u r) -> p g r u", g=G, u=U),
+            )
+            return grouped
+
+        def widen_attender(j):
+            nc.scalar.copy(out=a_rows[j][:], in_=codes_raw[:, j, :].bitcast(FP8))
+
+        def turn_attender(j):
+            bank = turn(a_rows[j][:])
+            pairs = bank[:].bitcast(BF16).rearrange("p (g u r e) -> p g r u e", g=G, u=U, e=2)
+            r0 = (j % (N2 // P)) * P
+            for g in range(G):
+                nc.vector.tensor_tensor(
+                    out=a_wide[j // (N2 // P)][:, g, r0 : r0 + P, :].rearrange("p r (u e) -> p r u e", u=U),
+                    in0=pairs[:, g],
+                    in1=scale[:, g, :].rearrange("p (o u e) -> p o u e", o=1, u=U).to_broadcast([P, P, U, 2]),
+                    op=MULT,
+                )
+
+        def quantise_attender(h):
+            for g in range(G):
+                quantise(a_q[h][g], a_wide[h][:, g].rearrange("p r t -> p (r t)"))
+
+        def first_matmuls(i):
+            weights = w_q[0] if i < S_TILES else w_q[1]
+            banks = []
+            for g in range(G):
+                bank = first_psum.tile([P, T * P], F32, name="first")
+                for t in range(T):
+                    codes, planes = weights[g * T + t]
+                    for k in range(G):
+                        cols = slice(k * P, (k + 1) * P)
+                        nc.tensor.matmul_mx(
+                            out=bank[:, t * P : (t + 1) * P],
+                            lhsT=codes[:, cols].bitcast(FP8X4),
+                            lhsT_scale=planes[:, cols],
+                            rhs=x_q[i][0][:, cols].bitcast(FP8X4),
+                            rhs_scale=x_q[i][1][:, cols],
+                            start=(k == 0),
+                            stop=(k == G - 1),
+                        )
+                banks.append(bank)
+            return banks
+
+        def add_bias(i, banks):
+            b = bias[0] if i < S_TILES else bias[1]
+            grouped = sums.tile([P, G, P, T], BF16, name="p_grouped", align_bytes=64)
+            for g in range(G):
+                nc.vector.tensor_tensor(
+                    out=grouped[:, g],
+                    in0=banks[g][:].rearrange("p (t r) -> p r t", t=T),
+                    in1=b[:, g, :].rearrange("p (o t) -> p o t", o=1).to_broadcast([P, P, T]),
+                    op=ADD,
+                )
+            return grouped
+
+        def second_matmuls(i, h):
+            bank = second_psum.tile([P, N2], F32, name="second")
+            for g in range(G):
+                cols = slice(g * P, (g + 1) * P)
+                nc.tensor.matmul_mx(
+                    out=bank[:],
+                    lhsT=p_q[i][0][:, cols].bitcast(FP8X4),
+                    lhsT_scale=p_q[i][1][:, cols],
+                    rhs=a_q[h][g][0][:].bitcast(FP8X4),
+                    rhs_scale=a_q[h][g][1][:],
+                    start=(g == 0),
+                    stop=(g == G - 1),
+                )
+            return bank
+
+        out_s = out_0.rearrange("(q p e) m -> p q e m", p=P, e=2)
+        out_e = out_1.rearrange("(q p e) m -> p q e m", p=P, e=2)
+
+        def scores(i, h, copy):
+            bank = second_matmuls(i, h)
+            result = results.tile([P, N2], F32, name="result")
+            copy(out=result[:], in_=bank[:])
+            rows = out_s[:, i // 2, i % 2] if i < S_TILES else out_e[:, (i - S_TILES) // 2, i % 2]
+            nc.sync.dma_start(out=rows[:, h * N2 : (h + 1) * N2], in_=result[:])
+
+        waiting = []
+        sorted_rows = {}
+
+        def quantise_waiting(limit):
+            while len(waiting) > limit:
+                dst, grouped = waiting.pop(0)
+                quantise(dst, grouped[:])
+
+        def raw(key):
+            kind, j = key
+            return x_raw[:, j, :] if kind == "x" else w_raw[kind][:, j, :]
+
+        def turn_tile(key):
+            kind, j = key
+            if kind == "a":
+                turn_attender(j)
+                return
+            dst = x_q[j] if kind == "x" else w_q[kind][j]
+            waiting.append((dst, turn_plain(key, raw(key))))
+
+        PRO = [(0, 0), (0, 1), ("a", 0), (0, 2), (0, 3), (0, 4), ("a", 1), (0, 5), ("x", 0), (0, 6), (0, 7)]
+        STEPS = [
+            ([("a", 2), ("x", 1)], -1, [], [("S", ("x", 2)), ("S", (1, 0))]),
+            ([("a", 3), ("x", 2), (1, 0)], 0, [], [("S", ("x", 3)), ("S", (1, 1))]),
+            ([("a", 4), ("x", 3), (1, 1)], -1, [(0, 0)], [("S", ("x", 4)), ("S", (1, 2))]),
+            ([("a", 5), ("x", 4), (1, 2)], -1, [(1, 0), (2, 0)], [("S", ("x", 5)), ("S", (1, 3))]),
+            ([("a", 6), ("x", 5), (1, 3)], -1, [(3, 0)], [("S", ("x", 6)), ("S", (1, 4)), ("V", (1, 5))]),
+            ([("a", 7), ("x", 6), (1, 4), (1, 5)], 1, [(4, 0)], [("S", ("x", 7)), ("S", ("x", 8)), ("V", (1, 6)), ("V", (1, 7))]),
+            ([("x", 7), ("x", 8), (1, 6), (1, 7)], -1, [(5, 0),(5,1)], [("S", ("x", 9)), ("V", ("x", 10)), ("V", ("x", 11))]),
+            ([("x", 9), ("x", 10), ("x", 11)], -1, [(6, 0), (6, 1), (0, 1), (1, 1)], []),
+            ([], -1, [(7, 0), (7, 1), (2, 1)], []),
+            ([], -1, [(8, 0), (8, 1), (3, 1)], []),
+            ([], -1, [(9, 0), (9, 1), (4, 1)], []),
+            ([], -1, [(10, 0), (10, 1)], []),
+            ([], -1, [(11, 0), (11, 1)], []),
+        ]
+        widened = 0
+        for n in range(2):
+            widen_attender(widened)
+            widened += 1
+        for n, key in enumerate(PRO):
+            if isinstance(key, str):
+                quantise_attender(0)
+                continue
+            turn_tile(key)
+            if key[0] == "a" and widened < 8:
+                widen_attender(widened)
+                widened += 1
+            quantise_waiting(1)
+        for i, (tiles, qa, units, sorts) in enumerate(STEPS):
+            for key in tiles:
+                turn_tile(key)
+                if key[0] == "a" and widened < 8:
+                    widen_attender(widened)
+                    widened += 1
+            if qa >= 0:
+                quantise_attender(qa)
+            quantise_waiting(1)
+            if i < TILES:
+                banks = first_matmuls(i)
+                grouped_p = add_bias(i, banks)
+            quantise_waiting(0)
+            for engine, key in sorts:
+                sorted_rows[key] = sort_words(engine, raw(key))
+            if i < TILES:
+                quantise(p_q[i], grouped_p[:].rearrange("p g r t -> p (g r t)"))
+            for n, (t, h) in enumerate(units):
+                scores(t, h, nc.vector.tensor_copy if i == TILES and n == 1 else nc.scalar.copy)

@@ -32,10 +32,10 @@ def tile_attention_pa_kernel(
     nc = tc.nc
     with ExitStack() as ctx:
         keep = ctx.enter_context(tc.tile_pool(name="keep", bufs=1))
-        wide = ctx.enter_context(tc.tile_pool(name="wide", bufs=4))
+        wide = ctx.enter_context(tc.tile_pool(name="wide", bufs=5))
         ordered_pool = ctx.enter_context(tc.tile_pool(name="ordered_pool", bufs=6))
         sums = ctx.enter_context(tc.tile_pool(name="sums", bufs=3))
-        results = ctx.enter_context(tc.tile_pool(name="results", bufs=4))
+        results = ctx.enter_context(tc.tile_pool(name="results", bufs=10))
         turn_psum = ctx.enter_context(tc.psum_pool(name="turn_psum", bufs=3))
         first_psum = ctx.enter_context(tc.psum_pool(name="first_psum", bufs=2))
         second_psum = ctx.enter_context(tc.psum_pool(name="second_psum", bufs=3))
@@ -44,8 +44,8 @@ def tile_attention_pa_kernel(
         ident = keep.tile([P, P], F32, name="ident")
         make_identity(nc, ident[:])
 
-        scale = keep.tile([P, G, T], F32, name="scale")
-        nc.scalar.dma_start(out=scale[:], in_=attender_scale.rearrange("o (g p t) -> p (o g) t", g=G, p=P, t=T))
+        scale_columns = keep.tile([P, G, T], F32, name="scale_columns")
+        nc.scalar.dma_start(out=scale_columns[:], in_=attender_scale.rearrange("o (g n c) -> n (o g) c", g=G, c=T))
         bias = []
         for name, vec in (("bias_ss", b_ss), ("bias_es", b_es)):
             b = keep.tile([P, G, T], BF16, name=name)
@@ -78,19 +78,20 @@ def tile_attention_pa_kernel(
         load_bytes(0, 2)
         load_weight(0, 1, 1)
         load_weight(0, 2, 2)
-        load_bytes(2, 2)
         load_weight(0, 4, 2)
-        load_weight(0, 6, 2)
         load_rows(0)
-        load_bytes(4, 4)
+        load_weight(0, 6, 2)
+        load_bytes(2, 2)
         load_rows(2)
+        load_bytes(4, 2)
         load_weight(1, 0, 2)
         load_rows(4)
+        load_bytes(6, 2)
         load_weight(1, 2, 2)
-        load_weight(1, 4, 2)
         load_rows(6)
-        load_weight(1, 6, 2)
+        load_weight(1, 4, 2)
         load_rows(8)
+        load_weight(1, 6, 2)
         load_rows(10)
 
         def quantised(name, words):
@@ -108,53 +109,57 @@ def tile_attention_pa_kernel(
         def quantise(dst, src):
             nc.vector.quantize_mx(out=dst[0][:].bitcast(FP8X4), scales=dst[1][:], in_=src)
 
-        def turn(rows):
+        sorted_rows = {}
+
+        def raw(key):
+            kind, j = key
+            return {"x": x_raw, 0: w_raw[0], 1: w_raw[1]}[kind][:, j, :]
+
+        def sort_words(key, copy):
+            rows = ordered_pool.tile([P, H], BF16, name="ordered")
+            copy(
+                out=rows[:].bitcast(F32).rearrange("p (g u q) -> p g u q", g=G, u=U),
+                in_=raw(key).bitcast(F32).rearrange("p (g q u) -> p g u q", g=G, u=U),
+            )
+            sorted_rows[key] = rows
+
+        def turn(key, copy):
+            kind, j = key
             bank = turn_psum.tile([P, G * U * P], F32, name="turned")
+            is_sorted = key in sorted_rows
+            rows = sorted_rows.pop(key)[:] if is_sorted else a_rows[j][:] if kind == "a" else raw(key)
             words = rows.bitcast(F32)
             for g in range(G):
                 for u in range(U):
                     c = (g * U + u) * P
-                    nc.tensor.transpose(bank[:, c : c + P], words[:, 256 * g + u : 256 * (g + 1) : U], ident[:])
-            return bank
+                    cols = slice(c, c + P) if is_sorted else slice(2 * P * g + u, 2 * P * (g + 1), U)
+                    nc.tensor.transpose(bank[:, c : c + P], words[:, cols], ident[:])
+            if kind == "a":
+                r0 = j % (N2 // P) * P
+                grouped = a_wide[j // (N2 // P)][:].rearrange("p g r t -> p (g r t)").bitcast(F32)
+                grouped = grouped.rearrange("p (g r u) -> p g r u", g=G, u=U)[:, :, r0 : r0 + P, :]
+            else:
+                tile = wide.tile([P, G * P * T], BF16, name="grouped", align_bytes=64)
+                grouped = tile[:].bitcast(F32).rearrange("p (g r u) -> p g r u", g=G, u=U)
+                waiting.append((x_q[j] if kind == "x" else w_q[kind][j], tile))
+            copy(out=grouped, in_=bank[:].rearrange("p (g u r) -> p g r u", g=G, u=U))
 
-        def turn_sorted(rows):
+        scale_spread = keep.tile([P, H], F32, name="scale_spread")
+
+        def spread_scale(g, copy):
             bank = turn_psum.tile([P, G * U * P], F32, name="turned")
-            words = rows.bitcast(F32)
-            for c in range(0, G * U * P, P):
-                nc.tensor.transpose(bank[:, c : c + P], words[:, c : c + P], ident[:])
-            return bank
-
-        def sort_words(engine, rows):
-            ordered = ordered_pool.tile([P, H], BF16, name="ordered")
-            (nc.vector.tensor_copy if engine == "V" else nc.scalar.copy)(
-                out=ordered[:].bitcast(F32).rearrange("p (g u q) -> p g u q", g=G, u=U),
-                in_=rows.bitcast(F32).rearrange("p (g q u) -> p g u q", g=G, u=U),
+            for c in range(T):
+                column = scale_columns[:, g, c : c + 1].to_broadcast([P, P])
+                nc.tensor.transpose(bank[:, c * P : (c + 1) * P], column, ident[:])
+            copy(
+                out=scale_spread[:, g * P * T : (g + 1) * P * T].rearrange("p (n c) -> p n c", c=T),
+                in_=bank[:].rearrange("p (c n) -> p n c", c=T),
             )
-            return ordered
 
-        def turn_plain(key, rows):
-            bank = turn_sorted(sorted_rows.pop(key)[:]) if key in sorted_rows else turn(rows)
-            grouped = wide.tile([P, G * P * T], BF16, name="grouped", align_bytes=64)
-            nc.scalar.copy(
-                out=grouped[:].bitcast(F32).rearrange("p (g r u) -> p g r u", g=G, u=U),
-                in_=bank[:].rearrange("p (g u r) -> p g r u", g=G, u=U),
+        def scale_attender(j):
+            nc.vector.tensor_tensor(
+                out=a_rows[j][:], in0=codes_raw[:, j, :].bitcast(FP8), in1=scale_spread[:], op=MULT
             )
-            return grouped
-
-        def widen_attender(j):
-            nc.scalar.copy(out=a_rows[j][:], in_=codes_raw[:, j, :].bitcast(FP8))
-
-        def turn_attender(j):
-            bank = turn(a_rows[j][:])
-            pairs = bank[:].bitcast(BF16).rearrange("p (g u r e) -> p g r u e", g=G, u=U, e=2)
-            r0 = (j % (N2 // P)) * P
-            for g in range(G):
-                nc.vector.tensor_tensor(
-                    out=a_wide[j // (N2 // P)][:, g, r0 : r0 + P, :].rearrange("p r (u e) -> p r u e", u=U),
-                    in0=pairs[:, g],
-                    in1=scale[:, g, :].rearrange("p (o u e) -> p o u e", o=1, u=U).to_broadcast([P, P, U, 2]),
-                    op=MULT,
-                )
 
         def quantise_attender(h):
             for g in range(G):
@@ -219,70 +224,66 @@ def tile_attention_pa_kernel(
             nc.sync.dma_start(out=rows[:, h * N2 : (h + 1) * N2], in_=result[:])
 
         waiting = []
-        sorted_rows = {}
 
         def quantise_waiting(limit):
             while len(waiting) > limit:
                 dst, grouped = waiting.pop(0)
                 quantise(dst, grouped[:])
 
-        def raw(key):
-            kind, j = key
-            return x_raw[:, j, :] if kind == "x" else w_raw[kind][:, j, :]
-
-        def turn_tile(key):
-            kind, j = key
-            if kind == "a":
-                turn_attender(j)
-                return
-            dst = x_q[j] if kind == "x" else w_q[kind][j]
-            waiting.append((dst, turn_plain(key, raw(key))))
-
-        PRO = [(0, 0), (0, 1), ("a", 0), (0, 2), (0, 3), (0, 4), ("a", 1), (0, 5), ("x", 0), (0, 6), (0, 7)]
-        STEPS = [
-            ([("a", 2), ("x", 1)], -1, [], [("S", ("x", 2)), ("S", (1, 0))]),
-            ([("a", 3), ("x", 2), (1, 0)], 0, [], [("S", ("x", 3)), ("S", (1, 1))]),
-            ([("a", 4), ("x", 3), (1, 1)], -1, [(0, 0)], [("S", ("x", 4)), ("S", (1, 2))]),
-            ([("a", 5), ("x", 4), (1, 2)], -1, [(1, 0), (2, 0)], [("S", ("x", 5)), ("S", (1, 3))]),
-            ([("a", 6), ("x", 5), (1, 3)], -1, [(3, 0)], [("S", ("x", 6)), ("S", (1, 4)), ("V", (1, 5))]),
-            ([("a", 7), ("x", 6), (1, 4), (1, 5)], 1, [(4, 0)], [("S", ("x", 7)), ("S", ("x", 8)), ("V", (1, 6)), ("V", (1, 7))]),
-            ([("x", 7), ("x", 8), (1, 6), (1, 7)], -1, [(5, 0),(5,1)], [("S", ("x", 9)), ("V", ("x", 10)), ("V", ("x", 11))]),
-            ([("x", 9), ("x", 10), ("x", 11)], -1, [(6, 0), (6, 1), (0, 1), (1, 1)], []),
-            ([], -1, [(7, 0), (7, 1), (2, 1)], []),
-            ([], -1, [(8, 0), (8, 1), (3, 1)], []),
-            ([], -1, [(9, 0), (9, 1), (4, 1)], []),
-            ([], -1, [(10, 0), (10, 1)], []),
-            ([], -1, [(11, 0), (11, 1)], []),
-        ]
-        widened = 0
-        for n in range(2):
-            widen_attender(widened)
-            widened += 1
-        for n, key in enumerate(PRO):
-            if isinstance(key, str):
+        on_scalar = nc.scalar.copy
+        on_vector = nc.vector.tensor_copy
+        AHALF = N2 // P
+        spread_scale(0, on_scalar)
+        spread_scale(1, on_vector)
+        for scaled in range(2):
+            scale_attender(scaled)
+        scaled = 2
+        for key in [(0, 0), (0, 1), (0, 2), (0, 3), ("a", 0), (0, 4), (0, 5), ("a", 1), ("x", 0), (0, 6), (0, 7), ("x", 1)]:
+            turn(key, on_scalar)
+            quantise_waiting(0)
+            if key[0] == "a" and scaled < 4:
+                scale_attender(scaled)
+                scaled += 1
+        while scaled < 4:
+            scale_attender(scaled)
+            scaled += 1
+        units = {
+            3: [(0, 0), (1, 0)],
+            4: [(2, 0)],
+            5: [(3, 0)],
+            6: [(4, 0), (5, 0)],
+            7: [(6, 0), (0, 1)],
+            8: [(7, 0), (1, 1), (2, 1)],
+            9: [(8, 0), (3, 1), (4, 1), (5, 1)],
+            10: [(9, 0), (6, 1), (7, 1)],
+            11: [(10, 0), (8, 1), (9, 1)],
+            12: [(10, 1), (11, 0), (11, 1)],
+        }
+        scaled_in = {0: 4, 1: 5, 3: 6, 4: 7}
+        for i in range(TILES + 1):
+            if i < 6:
+                turn(("a", i + 2), on_scalar)
+            if i < TILES - 2:
+                turn(("x", i + 2), on_scalar)
+            if i < G * T:
+                turn((1, i), on_scalar)
+            if i in scaled_in:
+                scale_attender(scaled_in[i])
+            sorter = on_vector if i >= 5 else on_scalar
+            if 1 <= i < TILES - 3:
+                sort_words(("x", i + 3), sorter)
+            if 1 <= i < G * T - 1:
+                sort_words((1, i + 1), sorter)
+            quantise_waiting(1)
+            if i == 2:
                 quantise_attender(0)
-                continue
-            turn_tile(key)
-            if key[0] == "a" and widened < 8:
-                widen_attender(widened)
-                widened += 1
-            quantise_waiting(1)
-        for i, (tiles, qa, units, sorts) in enumerate(STEPS):
-            for key in tiles:
-                turn_tile(key)
-                if key[0] == "a" and widened < 8:
-                    widen_attender(widened)
-                    widened += 1
-            if qa >= 0:
-                quantise_attender(qa)
-            quantise_waiting(1)
+            if i == 6:
+                quantise_attender(1)
             if i < TILES:
                 banks = first_matmuls(i)
                 grouped_p = add_bias(i, banks)
             quantise_waiting(0)
-            for engine, key in sorts:
-                sorted_rows[key] = sort_words(engine, raw(key))
+            for t, h in units.get(i, []):
+                scores(t, h, on_vector if (t, h) == (TILES - 1, 1) else on_scalar)
             if i < TILES:
                 quantise(p_q[i], grouped_p[:].rearrange("p g r t -> p (g r t)"))
-            for n, (t, h) in enumerate(units):
-                scores(t, h, nc.vector.tensor_copy if i == TILES and n == 1 else nc.scalar.copy)

@@ -44,6 +44,14 @@ def tile_attention_pa_kernel(
         ident = keep.tile([P, P], F32, name="ident")
         make_identity(nc, ident[:])
 
+        zeros = keep.tile([P, N2], BF16, name="zeros")
+        nc.vector.memset(zeros[:], 0.0)
+
+        def keep_warm(n):
+            bank = second_psum.tile([P, N2], F32, name="second")
+            for dummy in range(n):
+                nc.tensor.matmul(bank[:], lhsT=zeros[:, :P], rhs=zeros[:], start=True, stop=True)
+
         scale_columns = keep.tile([P, G, T], F32, name="scale_columns")
         nc.scalar.dma_start(out=scale_columns[:], in_=attender_scale.rearrange("o (g n c) -> n (o g) c", g=G, c=T))
         bias = []
@@ -165,38 +173,35 @@ def tile_attention_pa_kernel(
             for g in range(G):
                 quantise(a_q[h][g], a_wide[h][:, g].rearrange("p r t -> p (r t)"))
 
-        def first_matmuls(i):
-            weights = w_q[0] if i < S_TILES else w_q[1]
-            banks = []
-            for g in range(G):
-                bank = first_psum.tile([P, T * P], F32, name="first")
-                for t in range(T):
-                    codes, planes = weights[g * T + t]
-                    for k in range(G):
-                        cols = slice(k * P, (k + 1) * P)
-                        nc.tensor.matmul_mx(
-                            out=bank[:, t * P : (t + 1) * P],
-                            lhsT=codes[:, cols].bitcast(FP8X4),
-                            lhsT_scale=planes[:, cols],
-                            rhs=x_q[i][0][:, cols].bitcast(FP8X4),
-                            rhs_scale=x_q[i][1][:, cols],
-                            start=(k == 0),
-                            stop=(k == G - 1),
-                        )
-                banks.append(bank)
-            return banks
+        p_grouped = {}
 
-        def add_bias(i, banks):
-            b = bias[0] if i < S_TILES else bias[1]
-            grouped = sums.tile([P, G, P, T], BF16, name="p_grouped", align_bytes=64)
-            for g in range(G):
-                nc.vector.tensor_tensor(
-                    out=grouped[:, g],
-                    in0=banks[g][:].rearrange("p (t r) -> p r t", t=T),
-                    in1=b[:, g, :].rearrange("p (o t) -> p o t", o=1).to_broadcast([P, P, T]),
-                    op=ADD,
-                )
-            return grouped
+        def project(i, g):
+            bank = first_psum.tile([P, T * P], F32, name="first")
+            for t in range(T):
+                codes, planes = w_q[0 if i < S_TILES else 1][g * T + t]
+                for k in range(G):
+                    cols = slice(k * P, (k + 1) * P)
+                    nc.tensor.matmul_mx(
+                        out=bank[:, t * P : (t + 1) * P],
+                        lhsT=codes[:, cols].bitcast(FP8X4),
+                        lhsT_scale=planes[:, cols],
+                        rhs=x_q[i][0][:, cols].bitcast(FP8X4),
+                        rhs_scale=x_q[i][1][:, cols],
+                        start=(k == 0),
+                        stop=(k == G - 1),
+                    )
+            if i not in p_grouped:
+                p_grouped[i] = sums.tile([P, G, P, T], BF16, name="p_grouped", align_bytes=64)
+            b = bias[0 if i < S_TILES else 1]
+            nc.vector.tensor_tensor(
+                out=p_grouped[i][:, g],
+                in0=bank[:].rearrange("p (t r) -> p r t", t=T),
+                in1=b[:, g, :].rearrange("p (o t) -> p o t", o=1).to_broadcast([P, P, T]),
+                op=ADD,
+            )
+
+        def quantise_p(i):
+            quantise(p_q[i], p_grouped.pop(i)[:].rearrange("p g r t -> p (g r t)"))
 
         def second_matmuls(i, h):
             bank = second_psum.tile([P, N2], F32, name="second")
@@ -232,14 +237,18 @@ def tile_attention_pa_kernel(
 
         on_scalar = nc.scalar.copy
         on_vector = nc.vector.tensor_copy
-        AHALF = N2 // P
+        keep_warm(7)
         spread_scale(0, on_scalar)
         spread_scale(1, on_vector)
         for scaled in range(2):
             scale_attender(scaled)
         scaled = 2
-        for key in [(0, 0), (0, 1), (0, 2), (0, 3), ("a", 0), (0, 4), (0, 5), ("a", 1), ("x", 0), (0, 6), (0, 7), ("x", 1)]:
-            turn(key, on_scalar)
+        vev = []
+        dum = {1: 2, 3: 2, 5: 2, 7: 2, 9: 2, 11: 2}
+        for n, key in enumerate([(0, 0), (0, 1), (0, 2), (0, 3), ("a", 0), (0, 4), (0, 5), ("a", 1), ("x", 0), (0, 6), (0, 7), ("x", 1)]):
+            if n in dum:
+                keep_warm(dum[n])
+            turn(key, on_vector if key in vev else on_scalar)
             quantise_waiting(0)
             if key[0] == "a" and scaled < 4:
                 scale_attender(scaled)
@@ -247,43 +256,39 @@ def tile_attention_pa_kernel(
         while scaled < 4:
             scale_attender(scaled)
             scaled += 1
-        units = {
-            3: [(0, 0), (1, 0)],
-            4: [(2, 0)],
-            5: [(3, 0)],
-            6: [(4, 0), (5, 0)],
-            7: [(6, 0), (0, 1)],
-            8: [(7, 0), (1, 1), (2, 1)],
-            9: [(8, 0), (3, 1), (4, 1), (5, 1)],
-            10: [(9, 0), (6, 1), (7, 1)],
-            11: [(10, 0), (8, 1), (9, 1)],
-            12: [(10, 1), (11, 0), (11, 1)],
-        }
+        units = {3: [(0, 0), (1, 0)], 4: [(2, 0)], 5: [(3, 0)], 6: [(4, 0), (5, 0)], 7: [(6, 0), (0, 1)], 8: [(7, 0), (1, 1), (2, 1)], 9: [(8, 0), (3, 1), (4, 1), (5, 1)], 10: [(9, 0), (6, 1), (7, 1)], 11: [(10, 0), (8, 1), (9, 1)], 12: [(10, 1), (11, 0), (11, 1)]}
         scaled_in = {0: 4, 1: 5, 3: 6, 4: 7}
+        dstep = {}
+        sorts = {0: [("S", ("x", 3)), ("S", (1, 1))], 1: [("S", ("x", 4)), ("S", (1, 2))], 2: [("S", ("x", 5)), ("S", (1, 3))], 3: [("S", ("x", 6)), ("S", (1, 4))], 4: [("S", ("x", 7)), ("S", (1, 5))], 5: [("V", ("x", 8)), ("V", (1, 6))], 6: [("V", ("x", 9)), ("V", (1, 7))], 7: [("V", ("x", 10))], 8: [("V", ("x", 11))]}
+        turns = {0: [("a", 2), ("x", 2), (1, 0)], 1: [("a", 3), ("x", 3), (1, 1)], 2: [("a", 4), ("x", 4), (1, 2)], 3: [("a", 5), ("x", 5), (1, 3)], 4: [("a", 6), ("x", 6), (1, 4)], 5: [("a", 7), ("x", 7), (1, 5)], 6: [("x", 8), (1, 6)], 7: [("x", 9), (1, 7)], 8: [("x", 10)], 9: [("x", 11)]}
         for i in range(TILES + 1):
-            if i < 6:
-                turn(("a", i + 2), on_scalar)
-            if i < TILES - 2:
-                turn(("x", i + 2), on_scalar)
-            if i < G * T:
-                turn((1, i), on_scalar)
+            tl = turns.get(i, [])
+            split = -1 > i
+            for key in tl[: 1 if split else 9]:
+                turn(key, on_scalar)
+            if i in dstep:
+                keep_warm(dstep[i])
             if i in scaled_in:
                 scale_attender(scaled_in[i])
-            sorter = on_vector if i >= 5 else on_scalar
-            if 1 <= i < TILES - 3:
-                sort_words(("x", i + 3), sorter)
-            if 1 <= i < G * T - 1:
-                sort_words((1, i + 1), sorter)
-            quantise_waiting(1)
+            for e, key in sorts.get(i, []):
+                sort_words(key, on_vector if e == "V" else on_scalar)
+            if split:
+                project(i, 0)
+                for key in tl[1:]:
+                    turn(key, on_scalar)
+                quantise_waiting(1)
+                project(i, 1)
+            else:
+                quantise_waiting(1)
             if i == 2:
                 quantise_attender(0)
             if i == 6:
                 quantise_attender(1)
-            if i < TILES:
-                banks = first_matmuls(i)
-                grouped_p = add_bias(i, banks)
+            if i < TILES and not split:
+                project(i, 0)
+                project(i, 1)
             quantise_waiting(0)
             for t, h in units.get(i, []):
-                scores(t, h, on_vector if (t, h) == (TILES - 1, 1) else on_scalar)
+                scores(t, h, on_vector if (t, h) in [(11, 1)] else on_scalar)
             if i < TILES:
-                quantise(p_q[i], grouped_p[:].rearrange("p g r t -> p (g r t)"))
+                quantise_p(i)

from contextlib import ExitStack

import concourse.mybir as mybir
from concourse.masks import make_identity

H, NS, NE, M = 1024, 1024, 512, 1024
FLOPS = 2 * (NS + NE) * H * H + 2 * (NS + NE) * M * H

F32 = mybir.dt.float32
BF16 = mybir.dt.bfloat16
U32 = mybir.dt.uint32
U8 = mybir.dt.uint8
FP8 = mybir.dt.float8_e4m3fn
FP8X4 = mybir.dt.float8_e4m3fn_x4
ADD = mybir.AluOpType.add
MULT = mybir.AluOpType.mult

P = 128
T = 4
G = H // (P * T)
U = 2
N2 = 512
HALVES = M // N2
S_TILES = NS // P
E_TILES = NE // P
TILES = S_TILES + E_TILES


def tile_attention_pa_kernel(
    tc, attendee_stmts, attendee_eres, attender_bytes, attender_scale, W_ss, b_ss, W_es, b_es, out_0, out_1
):
    nc = tc.nc
    with ExitStack() as ctx:
        keep = ctx.enter_context(tc.tile_pool(name="keep", bufs=1))
        wide = ctx.enter_context(tc.tile_pool(name="wide", bufs=5))
        ordered_pool = ctx.enter_context(tc.tile_pool(name="ordered_pool", bufs=6))
        sums = ctx.enter_context(tc.tile_pool(name="sums", bufs=3))
        results = ctx.enter_context(tc.tile_pool(name="results", bufs=10))
        turn_psum = ctx.enter_context(tc.psum_pool(name="turn_psum", bufs=3))
        first_psum = ctx.enter_context(tc.psum_pool(name="first_psum", bufs=2))
        second_psum = ctx.enter_context(tc.psum_pool(name="second_psum", bufs=3))
        ctx.enter_context(tc.manual_schedule())

        ident = keep.tile([P, P], F32, name="ident")
        make_identity(nc, ident[:])

        zeros = keep.tile([P, N2], BF16, name="zeros")
        nc.vector.memset(zeros[:], 0.0)

        def keep_warm(n):
            bank = second_psum.tile([P, N2], F32, name="second")
            for dummy in range(n):
                nc.tensor.matmul(bank[:], lhsT=zeros[:, :P], rhs=zeros[:], start=True, stop=True)

        scale_columns = keep.tile([P, G, T], F32, name="scale_columns")
        nc.scalar.dma_start(out=scale_columns[:], in_=attender_scale.rearrange("o (g n c) -> n (o g) c", g=G, c=T))
        bias = []
        for name, vec in (("bias_ss", b_ss), ("bias_es", b_es)):
            b = keep.tile([P, G, T], BF16, name=name)
            nc.scalar.dma_start(out=b[:], in_=vec.rearrange("(g p t) -> p g t", g=G, p=P, t=T))
            bias.append(b)

        codes_raw = keep.tile([P, M // P, H], U8, name="codes_raw")
        bytes_view = attender_bytes.rearrange("(j p) k -> p j k", p=P)
        w_raw = []
        w_view = []
        for name, w in (("w_ss_raw", W_ss), ("w_es_raw", W_es)):
            raw = keep.tile([P, G * T, H], BF16, name=name)
            w_raw.append(raw)
            w_view.append(w.rearrange("(g m t) k -> m g t k", g=G, m=P, t=T))
        x_raw = keep.tile([P, TILES, H], BF16, name="x_raw")
        s_view = attendee_stmts.rearrange("(q p e) k -> p q e k", p=P, e=2)
        e_view = attendee_eres.rearrange("(q p e) k -> p q e k", p=P, e=2)

        def load_bytes(j, n):
            nc.sync.dma_start(out=codes_raw[:, j : j + n, :], in_=bytes_view[:, j : j + n, :])

        def load_weight(w, j, n):
            nc.sync.dma_start(out=w_raw[w][:, j : j + n, :], in_=w_view[w][:, j // T, j % T : j % T + n, :])

        def load_rows(i):
            view = s_view[:, i // 2] if i < S_TILES else e_view[:, (i - S_TILES) // 2]
            nc.sync.dma_start(out=x_raw[:, i : i + 2, :], in_=view)

        load_weight(0, 0, 1)
        load_bytes(0, 2)
        load_weight(0, 1, 1)
        load_weight(0, 2, 2)
        load_weight(0, 4, 2)
        load_rows(0)
        load_weight(0, 6, 2)
        load_bytes(2, 2)
        load_rows(2)
        load_bytes(4, 2)
        load_weight(1, 0, 2)
        load_rows(4)
        load_bytes(6, 2)
        load_weight(1, 2, 2)
        load_rows(6)
        load_weight(1, 4, 2)
        load_rows(8)
        load_weight(1, 6, 2)
        load_rows(10)

        def quantised(name, words):
            codes = keep.tile([P, words], U32, name=name + "_codes", align_bytes=64)
            planes = keep.tile([P, words], U8, name=name + "_scales", align_bytes=64)
            return codes, planes

        w_q = [[quantised("w%d_%d" % (w, j), G * P) for j in range(G * T)] for w in range(2)]
        x_q = [quantised("x_%d" % i, G * P) for i in range(TILES)]
        p_q = [quantised("p_%d" % i, G * P) for i in range(TILES)]
        a_q = [[quantised("a_%d_%d" % (h, g), N2) for g in range(G)] for h in range(HALVES)]
        a_wide = [keep.tile([P, G, N2, T], BF16, name="a_wide_%d" % h, align_bytes=64) for h in range(HALVES)]
        a_rows = [keep.tile([P, H], BF16, name="a_rows_%d" % j) for j in range(M // P)]

        def quantise(dst, src):
            nc.vector.quantize_mx(out=dst[0][:].bitcast(FP8X4), scales=dst[1][:], in_=src)

        sorted_rows = {}

        def raw(key):
            kind, j = key
            return {"x": x_raw, 0: w_raw[0], 1: w_raw[1]}[kind][:, j, :]

        def sort_words(key, copy):
            rows = ordered_pool.tile([P, H], BF16, name="ordered")
            copy(
                out=rows[:].bitcast(F32).rearrange("p (g u q) -> p g u q", g=G, u=U),
                in_=raw(key).bitcast(F32).rearrange("p (g q u) -> p g u q", g=G, u=U),
            )
            sorted_rows[key] = rows

        def turn(key, copy):
            kind, j = key
            bank = turn_psum.tile([P, G * U * P], F32, name="turned")
            is_sorted = key in sorted_rows
            rows = sorted_rows.pop(key)[:] if is_sorted else a_rows[j][:] if kind == "a" else raw(key)
            words = rows.bitcast(F32)
            for g in range(G):
                for u in range(U):
                    c = (g * U + u) * P
                    cols = slice(c, c + P) if is_sorted else slice(2 * P * g + u, 2 * P * (g + 1), U)
                    nc.tensor.transpose(bank[:, c : c + P], words[:, cols], ident[:])
            if kind == "a":
                r0 = j % (N2 // P) * P
                grouped = a_wide[j // (N2 // P)][:].rearrange("p g r t -> p (g r t)").bitcast(F32)
                grouped = grouped.rearrange("p (g r u) -> p g r u", g=G, u=U)[:, :, r0 : r0 + P, :]
            else:
                tile = wide.tile([P, G * P * T], BF16, name="grouped", align_bytes=64)
                grouped = tile[:].bitcast(F32).rearrange("p (g r u) -> p g r u", g=G, u=U)
                waiting.append((x_q[j] if kind == "x" else w_q[kind][j], tile))
            copy(out=grouped, in_=bank[:].rearrange("p (g u r) -> p g r u", g=G, u=U))

        scale_spread = keep.tile([P, H], F32, name="scale_spread")

        def spread_scale(g, copy):
            bank = turn_psum.tile([P, G * U * P], F32, name="turned")
            for c in range(T):
                column = scale_columns[:, g, c : c + 1].to_broadcast([P, P])
                nc.tensor.transpose(bank[:, c * P : (c + 1) * P], column, ident[:])
            copy(
                out=scale_spread[:, g * P * T : (g + 1) * P * T].rearrange("p (n c) -> p n c", c=T),
                in_=bank[:].rearrange("p (c n) -> p n c", c=T),
            )

        def scale_attender(j):
            nc.vector.tensor_tensor(
                out=a_rows[j][:], in0=codes_raw[:, j, :].bitcast(FP8), in1=scale_spread[:], op=MULT
            )

        def quantise_attender(h):
            for g in range(G):
                quantise(a_q[h][g], a_wide[h][:, g].rearrange("p r t -> p (r t)"))

        p_grouped = {}

        def project(i, g):
            bank = first_psum.tile([P, T * P], F32, name="first")
            for t in range(T):
                codes, planes = w_q[0 if i < S_TILES else 1][g * T + t]
                for k in range(G):
                    cols = slice(k * P, (k + 1) * P)
                    nc.tensor.matmul_mx(
                        out=bank[:, t * P : (t + 1) * P],
                        lhsT=codes[:, cols].bitcast(FP8X4),
                        lhsT_scale=planes[:, cols],
                        rhs=x_q[i][0][:, cols].bitcast(FP8X4),
                        rhs_scale=x_q[i][1][:, cols],
                        start=(k == 0),
                        stop=(k == G - 1),
                    )
            if i not in p_grouped:
                p_grouped[i] = sums.tile([P, G, P, T], BF16, name="p_grouped", align_bytes=64)
            b = bias[0 if i < S_TILES else 1]
            nc.vector.tensor_tensor(
                out=p_grouped[i][:, g],
                in0=bank[:].rearrange("p (t r) -> p r t", t=T),
                in1=b[:, g, :].rearrange("p (o t) -> p o t", o=1).to_broadcast([P, P, T]),
                op=ADD,
            )

        def quantise_p(i):
            quantise(p_q[i], p_grouped.pop(i)[:].rearrange("p g r t -> p (g r t)"))

        def second_matmuls(i, h):
            bank = second_psum.tile([P, N2], F32, name="second")
            for g in range(G):
                cols = slice(g * P, (g + 1) * P)
                nc.tensor.matmul_mx(
                    out=bank[:],
                    lhsT=p_q[i][0][:, cols].bitcast(FP8X4),
                    lhsT_scale=p_q[i][1][:, cols],
                    rhs=a_q[h][g][0][:].bitcast(FP8X4),
                    rhs_scale=a_q[h][g][1][:],
                    start=(g == 0),
                    stop=(g == G - 1),
                )
            return bank

        out_s = out_0.rearrange("(q p e) m -> p q e m", p=P, e=2)
        out_e = out_1.rearrange("(q p e) m -> p q e m", p=P, e=2)

        def scores(i, h, copy):
            bank = second_matmuls(i, h)
            result = results.tile([P, N2], F32, name="result")
            copy(out=result[:], in_=bank[:])
            rows = out_s[:, i // 2, i % 2] if i < S_TILES else out_e[:, (i - S_TILES) // 2, i % 2]
            nc.sync.dma_start(out=rows[:, h * N2 : (h + 1) * N2], in_=result[:])

        waiting = []

        def quantise_waiting(limit):
            while len(waiting) > limit:
                dst, grouped = waiting.pop(0)
                quantise(dst, grouped[:])

        on_scalar = nc.scalar.copy
        on_vector = nc.vector.tensor_copy
        keep_warm(7)
        spread_scale(0, on_scalar)
        spread_scale(1, on_vector)
        for scaled in range(2):
            scale_attender(scaled)
        scaled = 2
        vev = []
        dum = {1: 2, 3: 2, 5: 2, 7: 2, 9: 2, 11: 2}
        for n, key in enumerate([(0, 0), (0, 1), (0, 2), (0, 3), ("a", 0), (0, 4), (0, 5), ("a", 1), ("x", 0), (0, 6), (0, 7), ("x", 1)]):
            if n in dum:
                keep_warm(dum[n])
            turn(key, on_vector if key in vev else on_scalar)
            quantise_waiting(0)
            if key[0] == "a" and scaled < 4:
                scale_attender(scaled)
                scaled += 1
        while scaled < 4:
            scale_attender(scaled)
            scaled += 1
        units = {3: [(0, 0), (1, 0)], 4: [(2, 0)], 5: [(3, 0)], 6: [(4, 0), (5, 0)], 7: [(6, 0), (0, 1)], 8: [(7, 0), (1, 1), (2, 1)], 9: [(8, 0), (3, 1), (4, 1), (5, 1)], 10: [(9, 0), (6, 1), (7, 1)], 11: [(10, 0), (8, 1), (9, 1)], 12: [(10, 1), (11, 0), (11, 1)]}
        scaled_in = {0: 4, 1: 5, 3: 6, 4: 7}
        dstep = {}
        sorts = {0: [("S", ("x", 3)), ("S", (1, 1))], 1: [("S", ("x", 4)), ("S", (1, 2))], 2: [("S", ("x", 5)), ("S", (1, 3))], 3: [("S", ("x", 6)), ("S", (1, 4))], 4: [("S", ("x", 7)), ("S", (1, 5))], 5: [("V", ("x", 8)), ("V", (1, 6))], 6: [("V", ("x", 9)), ("V", (1, 7))], 7: [("V", ("x", 10))], 8: [("V", ("x", 11))]}
        turns = {0: [("a", 2), ("x", 2), (1, 0)], 1: [("a", 3), ("x", 3), (1, 1)], 2: [("a", 4), ("x", 4), (1, 2)], 3: [("a", 5), ("x", 5), (1, 3)], 4: [("a", 6), ("x", 6), (1, 4)], 5: [("a", 7), ("x", 7), (1, 5)], 6: [("x", 8), (1, 6)], 7: [("x", 9), (1, 7)], 8: [("x", 10)], 9: [("x", 11)]}
        for i in range(TILES + 1):
            tl = turns.get(i, [])
            split = -1 > i
            for key in tl[: 1 if split else 9]:
                turn(key, on_scalar)
            if i in dstep:
                keep_warm(dstep[i])
            if i in scaled_in:
                scale_attender(scaled_in[i])
            for e, key in sorts.get(i, []):
                sort_words(key, on_vector if e == "V" else on_scalar)
            if split:
                project(i, 0)
                for key in tl[1:]:
                    turn(key, on_scalar)
                quantise_waiting(1)
                project(i, 1)
            else:
                quantise_waiting(1)
            if i == 2:
                quantise_attender(0)
            if i == 6:
                quantise_attender(1)
            if i < TILES and not split:
                project(i, 0)
                project(i, 1)
            quantise_waiting(0)
            for t, h in units.get(i, []):
                scores(t, h, on_vector if (t, h) in [(11, 1)] else on_scalar)
            if i < TILES:
                quantise_p(i)
